import numpy as np
import ml_dtypes


def mxq(x, axis, fmt="e4m3"):
    dtype, down = {"e4m3": (ml_dtypes.float8_e4m3fn, 7), "e5m2": (ml_dtypes.float8_e5m2, 14)}[fmt]
    v = np.moveaxis(np.asarray(x, np.float32).astype(ml_dtypes.bfloat16).astype(np.float64), axis, -1)
    blocks = v.reshape(v.shape[:-1] + (-1, 32))
    amax = np.abs(blocks).max(-1, keepdims=True)
    byte = np.maximum(np.where(amax > 0, np.frexp(amax)[1] - 1 + 127, 0) - down, 1)
    scale = np.exp2(byte - 127.0)
    codes = (blocks / scale).astype(np.float32).astype(dtype).astype(np.float64)
    return np.moveaxis((codes * scale).reshape(v.shape), -1, axis)


WIDE = False


def mx_kscale(k):
    if not WIDE:
        return np.ones(k)
    levels = np.array([10, -10, 5, -5, 0])
    if k % 512:
        return np.exp2(np.random.permutation(np.resize(levels, k // 32))).repeat(32)
    a = np.empty((k // 512, 16))
    for p in range(k // 512):
        a[p, :8] = np.random.permutation(np.resize(levels, 8))
        for g in range(8):
            far = levels[np.abs(levels - a[p, g]) >= 10]
            a[p, g + 8] = far[np.random.randint(len(far))]
    return np.exp2(a.ravel()).repeat(32)


BF16 = ml_dtypes.bfloat16


def bf(x):
    return np.asarray(x, np.float32).astype(BF16)


def f64(x):
    return np.asarray(x).astype(np.float64)


E2M1 = np.array([0.0, 0.5, 1.0, 1.5, 2.0, 3.0, 4.0, 6.0, -0.0, -0.5, -1.0, -1.5, -2.0, -3.0, -4.0, -6.0])


def pack_weight(w, fmt):
    k, n = w.shape
    w = f64(bf(w)).reshape(k // 32, 32, n)
    amax = np.abs(w).max(1)
    if fmt == "e4m3":
        byte = np.frexp(amax)[1] - 1 + 127 - 7
    else:
        mant, ex = np.frexp(amax / 6.0)
        byte = np.where(mant > 0.5, ex, ex - 1) + 127
    byte = np.clip(np.where(amax > 0, byte, 1), 1, 254)
    scaled = (w * np.exp2(127.0 - byte)[:, None, :]).reshape(k, n).astype(np.float32)
    by_word = np.ascontiguousarray(scaled.reshape(k // 512, 128, 4, n).transpose(0, 1, 3, 2))
    if fmt == "e4m3":
        words = by_word.astype(ml_dtypes.float8_e4m3fn).view(np.uint8)
    else:
        c = by_word.astype(ml_dtypes.float4_e2m1fn).view(np.uint8) & 0xF
        words = c[..., 0::2] | (c[..., 1::2] << 4)
    return np.ascontiguousarray(words), np.ascontiguousarray(byte.astype(np.uint8).reshape(k // 512, 16, n))


def unpack_weight(words, scales, fmt):
    g, p, n, _ = words.shape
    if fmt == "e4m3":
        vals = np.ascontiguousarray(words).view(ml_dtypes.float8_e4m3fn).astype(np.float64)
    else:
        nib = np.empty((g, p, n, 4), np.uint8)
        nib[..., 0::2] = words & 0xF
        nib[..., 1::2] = words >> 4
        vals = E2M1[nib]
    vals = vals * np.repeat(np.exp2(scales.astype(np.float64) - 127.0), 8, axis=1)[..., None]
    return vals.transpose(0, 1, 3, 2).reshape(g * 512, n)


B, N_EP, S, D, IN_DIM, L, K = 6, 3, 512, 256, 255, 512, 10


def draw0():
    s, t = mx_kscale(S), mx_kscale(L)
    r = np.random.standard_normal
    g = r((B, S, S)) * 1.56
    a = np.exp(g - g.max(-1, keepdims=True))
    a = a / a.sum(-1, keepdims=True)
    v1 = bf(r((B, S, L)) * 4.0 / s[:, None] * t)
    Wq2_words, Wq2_scales = pack_weight(r((L, L)) * 4.0 / np.sqrt(L) / t[:, None], "e4m3")
    bq2 = bf(r(L) * 0.2)
    Wk2_words, Wk2_scales = pack_weight(r((L, L)) * 4.0 / np.sqrt(L) / t[:, None], "e4m3")
    bk2 = bf(r(L) * 0.2)
    Wv2_words, Wv2_scales = pack_weight(r((L, L)) * 3.2 / np.sqrt(L) / t[:, None], "e4m3")
    bv2 = bf(r(L) * 0.2)
    return {"attn1": bf(a * s), "v1": v1,
            "Wq2_words": Wq2_words, "Wq2_scales": Wq2_scales, "bq2": bq2,
            "Wk2_words": Wk2_words, "Wk2_scales": Wk2_scales, "bk2": bk2,
            "Wv2_words": Wv2_words, "Wv2_scales": Wv2_scales, "bv2": bv2}


def core(attn1, v1, Wq2_words, Wq2_scales, bq2, Wk2_words, Wk2_scales, bk2, Wv2_words, Wv2_scales, bv2):
    h = np.maximum(mxq(f64(attn1), 2, "e4m3") @ mxq(f64(v1), 1, "e4m3"), 0.0)
    hq = mxq(h, 2, "e4m3")
    q2 = (hq @ unpack_weight(Wq2_words, Wq2_scales, "e4m3")) + f64(bq2)
    k2 = (hq @ unpack_weight(Wk2_words, Wk2_scales, "e4m3")) + f64(bk2)
    v2 = (hq @ unpack_weight(Wv2_words, Wv2_scales, "e4m3")) + f64(bv2)
    return q2, k2, v2


def e4m3fn_bytes(y):
    return np.clip(np.asarray(y, np.float64), -448.0, 448.0).astype(np.float32).astype(ml_dtypes.float8_e4m3fn).view(np.uint8)


def e4m3fn_values(b):
    return np.asarray(b, np.uint8).view(ml_dtypes.float8_e4m3fn).astype(np.float64)


def setup_inputs():
    d = draw0()
    x0 = np.asarray(d['attn1']).astype(np.float64)
    s = (np.max(np.abs(x0), axis=(0, 1), keepdims=True) / 448.0).astype(np.float32)
    out = {}
    for k, v in d.items():
        if k == 'attn1':
            out['attn1_bytes'] = e4m3fn_bytes(x0 / s.astype(np.float64))
            out['attn1_scale'] = s
        else:
            out[k] = v
    return out


def reference(attn1_bytes, attn1_scale, v1, Wq2_words, Wq2_scales, bq2, Wk2_words, Wk2_scales, bk2, Wv2_words, Wv2_scales, bv2):
    return core(e4m3fn_values(attn1_bytes) * attn1_scale.astype(np.float64), v1, Wq2_words, Wq2_scales, bq2, Wk2_words, Wk2_scales, bk2, Wv2_words, Wv2_scales, bv2)

@@ -1,0 +1,286 @@
+from contextlib import ExitStack
+
+import concourse.mybir as mybir
+from concourse.masks import make_identity
+
+SETS, POINTS, FEATS = 6, 512, 512
+FLOPS = 2 * SETS * POINTS * FEATS * (POINTS + 3 * FEATS)
+
+F32 = mybir.dt.float32
+BF16 = mybir.dt.bfloat16
+U8 = mybir.dt.uint8
+I32 = mybir.dt.int32
+FP8 = mybir.dt.float8_e4m3fn
+FP8X4 = mybir.dt.float8_e4m3fn_x4
+ADD = mybir.AluOpType.add
+MULT = mybir.AluOpType.mult
+COPY = mybir.ActivationFunctionType.Copy
+RELU = mybir.ActivationFunctionType.Relu
+
+P = 128
+PAIRS = 2 * SETS
+LATE = 8
+EARLY = 3
+
+
+def tile_perspectronencodernetwork_pa_w8_kernel(
+    tc, attn1_bytes, attn1_scale, v1,
+    wq_words, wq_scales, bq, wk_words, wk_scales, bk, wv_words, wv_scales, bv,
+    out_0, out_1, out_2,
+):
+    nc = tc.nc
+    outs = [out_0, out_1, out_2]
+    words_in = [wq_words, wk_words, wv_words]
+    wscales_in = [wq_scales, wk_scales, wv_scales]
+    biases_in = [bq, bk, bv]
+
+    with ExitStack() as ctx:
+        keep = ctx.enter_context(tc.tile_pool(name="keep", bufs=1))
+        work = ctx.enter_context(tc.tile_pool(name="work", bufs=3))
+        stores = ctx.enter_context(tc.tile_pool(name="stores", bufs=4))
+        ps_out = ctx.enter_context(tc.psum_pool(name="ps_out", bufs=4))
+        ps_h = ctx.enter_context(tc.psum_pool(name="ps_h", bufs=2))
+        ps_x = ctx.enter_context(tc.psum_pool(name="ps_x", bufs=2))
+        ctx.enter_context(tc.manual_schedule())
+
+        ident = keep.tile([P, P], F32)
+        make_identity(nc, ident[:])
+        warm = keep.tile([P, 1], F32)
+        nc.vector.memset(warm[:], 0.0)
+        bias_rows = keep.tile([P, 3 * FEATS], BF16)
+        nc.vector.memset(bias_rows[:].bitcast(F32), 0.0)
+        wscale_sb = keep.tile([P, 3 * FEATS], U8, align_bytes=64)
+        nc.vector.memset(wscale_sb[:].bitcast(I32), 0)
+        ones = keep.tile([P, P], BF16)
+        nc.vector.memset(ones[:], 1.0)
+        warm_out = keep.tile([P, 1], F32)
+        nc.scalar.activation(out=warm_out[:], in_=warm[:], func=RELU)
+
+        scale_col = keep.tile([P, 4], F32)
+        nc.sync.dma_start(out=scale_col[:], in_=attn1_scale.rearrange("a b (p t) -> p (a b t)", t=4))
+        codes_in = keep.tile([P, SETS, 4, POINTS], U8, align_bytes=64)
+        vraw = keep.tile([P, SETS, 4, FEATS], BF16, align_bytes=64)
+
+        def load_codes(b0, b1):
+            nc.sync.dma_start(out=codes_in[:, b0:b1], in_=attn1_bytes[b0:b1].rearrange("b (p r) s -> p b r s", r=4))
+
+        def load_v(b0, b1):
+            nc.sync.dma_start(out=vraw[:, b0:b1], in_=v1[b0:b1].rearrange("b (p j) f -> p b j f", j=4))
+
+        load_codes(0, 1)
+        load_v(0, 1)
+        load_codes(1, 2)
+        w_sb = keep.tile([P, 3, 4 * FEATS], U8, align_bytes=64)
+        for w in range(3):
+            nc.sync.dma_start(out=w_sb[:, w, :], in_=words_in[w][0].rearrange("p n t -> p (n t)"))
+        for w in range(3):
+            for quad in range(4):
+                nc.sync.dma_start(
+                    out=wscale_sb[32 * quad : 32 * quad + 4, FEATS * w : FEATS * (w + 1)].bitcast(I32),
+                    in_=wscales_in[w][0, 4 * quad : 4 * quad + 4, :].bitcast(I32),
+                )
+        for w in range(3):
+            nc.scalar.dma_start(out=bias_rows[0:1, FEATS * w : FEATS * (w + 1)], in_=biases_in[w].rearrange("(o n) -> o n", o=1))
+        load_v(1, 2)
+        load_codes(2, 6)
+        load_v(2, 4)
+        load_v(4, 6)
+
+        scale_ps = ps_x.tile([P, 4, P], F32, tag="x")
+        for t in range(4):
+            nc.tensor.transpose(scale_ps[:, t, :], scale_col[:, t : t + 1].to_broadcast([P, P]), ident[:])
+        scale_sb = keep.tile([P, POINTS], F32)
+        nc.scalar.copy(out=scale_sb[:].rearrange("q (p t) -> q p t", t=4), in_=scale_ps[:].rearrange("q t p -> q p t"))
+
+        bias_sb = keep.tile([P, 3, FEATS], F32)
+
+        def spread_bias(w):
+            ps = ps_out.tile([P, FEATS], F32, tag="o", name="bias_ps")
+            nc.tensor.matmul(ps[:], lhsT=ones[:], rhs=bias_rows[:, FEATS * w : FEATS * (w + 1)], start=True, stop=True)
+            nc.scalar.copy(out=bias_sb[:, w, :], in_=ps[:])
+
+        cast, prod, xt, xg, xq, xs = {}, {}, {}, {}, {}, {}
+        vg, vq, vs = {}, {}, {}
+        hps, hg, hq, hs = {}, {}, {}, {}
+
+        def do_cast(i):
+            if not EARLY <= i < PAIRS:
+                return
+            c = work.tile([P, 2, POINTS], BF16, tag="cast", name="cast_t")
+            cast[i] = c
+            h = 2 * (i % 2)
+            nc.scalar.copy(out=c[:], in_=codes_in[:, i // 2, h : h + 2, :].bitcast(FP8))
+
+        def do_prod(i, r=None):
+            if not 0 <= i < PAIRS:
+                return
+            if i not in prod:
+                y = work.tile([P, 2, POINTS], BF16, tag="prod", name="prod_t", align_bytes=64)
+                prod[i] = y
+            for k in (0, 1) if r is None else (r,):
+                if i < EARLY:
+                    nc.vector.tensor_tensor(out=prod[i][:, k, :], in0=codes_in[:, i // 2, 2 * (i % 2) + k, :].bitcast(FP8), in1=scale_sb[:], op=MULT)
+                else:
+                    nc.gpsimd.tensor_tensor(out=prod[i][:, k, :], in0=cast[i][:, k, :], in1=scale_sb[:], op=MULT)
+
+        def do_turn(i):
+            if not 0 <= i < PAIRS:
+                return
+            x = ps_x.tile([P, 2, 2, P], F32, tag="x", name="xt_t")
+            xt[i] = x
+            pairs_of_k = prod[i][:].rearrange("p r s -> p (r s)").bitcast(F32)
+            for r in range(2):
+                for u in range(2):
+                    nc.tensor.transpose(x[:, r, u, :], pairs_of_k[:, 256 * r + u : 256 * (r + 1) : 2], ident[:])
+
+        def do_group(i):
+            if not 0 <= i < PAIRS:
+                return
+            g = work.tile([P, 2 * P * 4], BF16, tag="xg", name="xg_t", align_bytes=64)
+            xg[i] = g
+            dst = g[:].bitcast(F32).rearrange("p (r q u) -> p r q u", r=2, u=2)
+            src = xt[i][:].rearrange("p r u q -> p r q u")
+            if i == 0:
+                nc.vector.tensor_copy(out=dst, in_=src)
+            else:
+                nc.scalar.copy(out=dst, in_=src)
+
+        def do_quant_x(i):
+            if not 0 <= i < PAIRS:
+                return
+            q = work.tile([P, 4 * 2 * P], U8, tag="xq", name="xq_t", align_bytes=64)
+            s = work.tile([P, 2 * P], U8, tag="xs", name="xs_t", align_bytes=64)
+            xq[i], xs[i] = q, s
+            nc.vector.quantize_mx(out=q[:].bitcast(FP8X4), scales=s[:], in_=xg[i][:])
+
+        def do_group_v(b, t):
+            if not 0 <= b < SETS:
+                return
+            if t == 0:
+                g = work.tile([P, 4, P, 4], BF16, tag="vg", name="vg_t", align_bytes=64)
+                vg[b] = g
+            nc.scalar.copy(out=vg[b][:, t], in_=vraw[:, b].rearrange("p j (m t) -> p t m j", t=4)[:, t])
+
+        def do_quant_v(b, half):
+            if not 0 <= b < SETS:
+                return
+            if half == 0:
+                q = work.tile([P, 4 * FEATS], U8, tag="vq", name="vq_t", align_bytes=64)
+                s = work.tile([P, FEATS], U8, tag="vs", name="vs_t", align_bytes=64)
+                vq[b], vs[b] = q, s
+            nc.vector.quantize_mx(
+                out=vq[b][:, 1024 * half : 1024 * (half + 1)].bitcast(FP8X4),
+                scales=vs[b][:, 256 * half : 256 * (half + 1)],
+                in_=vg[b][:, 2 * half : 2 * half + 2].rearrange("p t m j -> p (t m j)"),
+            )
+
+        def do_mix(i):
+            if not 0 <= i < PAIRS:
+                return
+            b = i // 2
+            for r in range(2):
+                h = ps_h.tile([P, 4, P], F32, tag="h", name="h_t")
+                hps[(i, r)] = h
+                for t in range(4):
+                    nc.tensor.matmul_mx(
+                        out=h[:, t, :],
+                        lhsT=vq[b][:, 512 * t : 512 * (t + 1)].bitcast(FP8X4),
+                        lhsT_scale=vs[b][:, P * t : P * (t + 1)],
+                        rhs=xq[i][:, 512 * r : 512 * (r + 1)].bitcast(FP8X4),
+                        rhs_scale=xs[i][:, P * r : P * (r + 1)],
+                        start=True, stop=True,
+                    )
+
+        def do_relu(i):
+            if not 0 <= i < PAIRS:
+                return
+            g = work.tile([P, 2, P, 4], BF16, tag="hg", name="hg_t", align_bytes=64)
+            hg[i] = g
+            for r in range(2):
+                nc.scalar.activation(out=g[:, r], in_=hps[(i, r)][:].rearrange("p t q -> p q t"), func=RELU)
+
+        def do_quant_h(i):
+            if not 0 <= i < PAIRS:
+                return
+            q = work.tile([P, 4 * 2 * P], U8, tag="hq", name="hq_t", align_bytes=64)
+            s = work.tile([P, 2 * P], U8, tag="hs", name="hs_t", align_bytes=64)
+            hq[i], hs[i] = q, s
+            nc.vector.quantize_mx(out=q[:].bitcast(FP8X4), scales=s[:], in_=hg[i][:].rearrange("p r q t -> p (r q t)"))
+
+        def do_project(i, w):
+            if not 0 <= i < PAIRS:
+                return
+            banks = []
+            for r in range(2):
+                o = ps_out.tile([P, FEATS], F32, tag="o", name="o_t")
+                banks.append(o)
+                nc.tensor.matmul_mx(
+                    out=o[:],
+                    lhsT=hq[i][:, 512 * r : 512 * (r + 1)].bitcast(FP8X4),
+                    lhsT_scale=hs[i][:, P * r : P * (r + 1)],
+                    rhs=w_sb[:, w, :].bitcast(FP8X4),
+                    rhs_scale=wscale_sb[:, FEATS * w : FEATS * (w + 1)],
+                    start=True, stop=True,
+                )
+            y = stores.tile([P, 2, FEATS], F32, tag="y%d" % w, name="y_t")
+            for r in range(2):
+                if r == 1 and w < 2 and i >= LATE:
+                    z = work.tile([P, FEATS], F32, tag="z", name="z_t")
+                    nc.scalar.copy(out=z[:], in_=banks[r][:])
+                    nc.gpsimd.tensor_tensor(out=y[:, r, :], in0=z[:], in1=bias_sb[:, w, :], op=ADD)
+                else:
+                    nc.vector.tensor_tensor(out=y[:, r, :], in0=banks[r][:], in1=bias_sb[:, w, :], op=ADD)
+            h = 2 * (i % 2)
+            rows = outs[w][i // 2].rearrange("(p r) n -> p r n", r=4)
+            if i == PAIRS - 1 and w == 2:
+                for r in range(2):
+                    nc.sync.dma_start(out=rows[:, h + r, :], in_=y[:, r, :])
+            else:
+                nc.sync.dma_start(out=rows[:, h : h + 2, :], in_=y[:])
+
+        do_prod(0)
+        do_turn(0)
+        for t in range(4):
+            do_group_v(0, t)
+        do_prod(1, 0)
+        do_group(0)
+        do_prod(1, 1)
+        do_quant_x(0)
+        do_turn(1)
+        do_quant_v(0, 0)
+        do_quant_v(0, 1)
+        do_mix(0)
+        for w in range(3):
+            spread_bias(w)
+        do_prod(2)
+        do_relu(0)
+        do_group(1)
+        do_cast(3)
+        do_quant_x(1)
+        do_quant_h(0)
+        do_mix(1)
+        do_prod(3)
+        for t in range(4):
+            do_group_v(1, t)
+        do_turn(2)
+        do_group(2)
+        do_cast(4)
+        do_quant_v(1, 0)
+        do_quant_v(1, 1)
+
+        for i in range(PAIRS):
+            do_relu(i + 1)
+            do_quant_x(i + 2)
+            do_project(i, 0)
+            do_turn(i + 3)
+            do_group(i + 3)
+            do_quant_h(i + 1)
+            do_project(i, 1)
+            b = i // 2 + 2
+            for t in (0, 1) if i % 2 == 0 else (2, 3):
+                do_group_v(b, t)
+            do_project(i, 2)
+            do_mix(i + 2)
+            do_quant_v(b, i % 2)
+            do_cast(i + 5)
+            do_prod(i + 4)

@@ -19,8 +19,8 @@ RELU = mybir.ActivationFunctionType.Relu
 
 P = 128
 PAIRS = 2 * SETS
-LATE = 8
-EARLY = 3
+EARLY = 4
+SHARED = {9: (1, 5), 10: (1,), 11: (1, 5)}
 
 
 def tile_perspectronencodernetwork_pa_w8_kernel(
@@ -36,8 +36,9 @@ def tile_perspectronencodernetwork_pa_w8_kernel(
 
     with ExitStack() as ctx:
         keep = ctx.enter_context(tc.tile_pool(name="keep", bufs=1))
-        work = ctx.enter_context(tc.tile_pool(name="work", bufs=3))
-        stores = ctx.enter_context(tc.tile_pool(name="stores", bufs=4))
+        work = ctx.enter_context(tc.tile_pool(name="work", bufs=4))
+        vwork = ctx.enter_context(tc.tile_pool(name="vwork", bufs=3))
+        stores = ctx.enter_context(tc.tile_pool(name="stores", bufs=5))
         ps_out = ctx.enter_context(tc.psum_pool(name="ps_out", bufs=4))
         ps_h = ctx.enter_context(tc.psum_pool(name="ps_h", bufs=2))
         ps_x = ctx.enter_context(tc.psum_pool(name="ps_x", bufs=2))
@@ -45,21 +46,24 @@ def tile_perspectronencodernetwork_pa_w8_kernel(
 
         ident = keep.tile([P, P], F32)
         make_identity(nc, ident[:])
-        warm = keep.tile([P, 1], F32)
-        nc.vector.memset(warm[:], 0.0)
         bias_rows = keep.tile([P, 3 * FEATS], BF16)
         nc.vector.memset(bias_rows[:].bitcast(F32), 0.0)
         wscale_sb = keep.tile([P, 3 * FEATS], U8, align_bytes=64)
         nc.vector.memset(wscale_sb[:].bitcast(I32), 0)
+        warm = keep.tile([P, 1], F32)
+        nc.vector.memset(warm[:], 0.0)
         ones = keep.tile([P, P], BF16)
         nc.vector.memset(ones[:], 1.0)
+
+        for w in range(3):
+            nc.scalar.dma_start(out=bias_rows[0:1, FEATS * w : FEATS * (w + 1)], in_=biases_in[w].rearrange("(o n) -> o n", o=1))
         warm_out = keep.tile([P, 1], F32)
         nc.scalar.activation(out=warm_out[:], in_=warm[:], func=RELU)
-
         scale_col = keep.tile([P, 4], F32)
         nc.sync.dma_start(out=scale_col[:], in_=attn1_scale.rearrange("a b (p t) -> p (a b t)", t=4))
         codes_in = keep.tile([P, SETS, 4, POINTS], U8, align_bytes=64)
         vraw = keep.tile([P, SETS, 4, FEATS], BF16, align_bytes=64)
+        w_sb = keep.tile([P, 3, 4 * FEATS], U8, align_bytes=64)
 
         def load_codes(b0, b1):
             nc.sync.dma_start(out=codes_in[:, b0:b1], in_=attn1_bytes[b0:b1].rearrange("b (p r) s -> p b r s", r=4))
@@ -67,24 +71,30 @@ def tile_perspectronencodernetwork_pa_w8_kernel(
         def load_v(b0, b1):
             nc.sync.dma_start(out=vraw[:, b0:b1], in_=v1[b0:b1].rearrange("b (p j) f -> p b j f", j=4))
 
-        load_codes(0, 1)
-        load_v(0, 1)
-        load_codes(1, 2)
-        w_sb = keep.tile([P, 3, 4 * FEATS], U8, align_bytes=64)
-        for w in range(3):
+        def load_words(w):
             nc.sync.dma_start(out=w_sb[:, w, :], in_=words_in[w][0].rearrange("p n t -> p (n t)"))
-        for w in range(3):
+
+        def load_wscales(w):
             for quad in range(4):
                 nc.sync.dma_start(
                     out=wscale_sb[32 * quad : 32 * quad + 4, FEATS * w : FEATS * (w + 1)].bitcast(I32),
                     in_=wscales_in[w][0, 4 * quad : 4 * quad + 4, :].bitcast(I32),
                 )
-        for w in range(3):
-            nc.scalar.dma_start(out=bias_rows[0:1, FEATS * w : FEATS * (w + 1)], in_=biases_in[w].rearrange("(o n) -> o n", o=1))
+
+        load_codes(0, 1)
+        load_v(0, 1)
+        load_wscales(0)
+        load_wscales(1)
+        load_codes(1, 2)
+        load_words(0)
+        load_words(1)
+        load_wscales(2)
+        load_words(2)
         load_v(1, 2)
-        load_codes(2, 6)
-        load_v(2, 4)
-        load_v(4, 6)
+        load_codes(2, 3)
+        load_v(2, 3)
+        load_codes(3, 6)
+        load_v(3, 6)
 
         scale_ps = ps_x.tile([P, 4, P], F32, tag="x")
         for t in range(4):
@@ -92,39 +102,40 @@ def tile_perspectronencodernetwork_pa_w8_kernel(
         scale_sb = keep.tile([P, POINTS], F32)
         nc.scalar.copy(out=scale_sb[:].rearrange("q (p t) -> q p t", t=4), in_=scale_ps[:].rearrange("q t p -> q p t"))
 
-        bias_sb = keep.tile([P, 3, FEATS], F32)
+        bias_sb = keep.tile([P, 3, FEATS], BF16)
 
-        def spread_bias(w):
-            ps = ps_out.tile([P, FEATS], F32, tag="o", name="bias_ps")
-            nc.tensor.matmul(ps[:], lhsT=ones[:], rhs=bias_rows[:, FEATS * w : FEATS * (w + 1)], start=True, stop=True)
-            nc.scalar.copy(out=bias_sb[:, w, :], in_=ps[:])
+        def spread_biases(w0, w1):
+            ps = ps_out.tile([P, 2, FEATS], BF16, tag="o", name="bias_ps")
+            for w in range(w0, w1):
+                nc.tensor.matmul(ps[:, w - w0, :], lhsT=ones[:], rhs=bias_rows[:, FEATS * w : FEATS * (w + 1)], start=True, stop=True)
+            nc.scalar.copy(out=bias_sb[:, w0:w1, :], in_=ps[:, : w1 - w0, :])
 
         cast, prod, xt, xg, xq, xs = {}, {}, {}, {}, {}, {}
         vg, vq, vs = {}, {}, {}
         hps, hg, hq, hs = {}, {}, {}, {}
+        bank, res, done = {}, {}, {}
 
         def do_cast(i):
-            if not EARLY <= i < PAIRS:
+            if i >= PAIRS:
                 return
             c = work.tile([P, 2, POINTS], BF16, tag="cast", name="cast_t")
             cast[i] = c
             h = 2 * (i % 2)
             nc.scalar.copy(out=c[:], in_=codes_in[:, i // 2, h : h + 2, :].bitcast(FP8))
 
-        def do_prod(i, r=None):
-            if not 0 <= i < PAIRS:
+        def do_prod(i, k):
+            if i >= PAIRS:
                 return
-            if i not in prod:
+            if k == 0:
                 y = work.tile([P, 2, POINTS], BF16, tag="prod", name="prod_t", align_bytes=64)
                 prod[i] = y
-            for k in (0, 1) if r is None else (r,):
-                if i < EARLY:
-                    nc.vector.tensor_tensor(out=prod[i][:, k, :], in0=codes_in[:, i // 2, 2 * (i % 2) + k, :].bitcast(FP8), in1=scale_sb[:], op=MULT)
-                else:
-                    nc.gpsimd.tensor_tensor(out=prod[i][:, k, :], in0=cast[i][:, k, :], in1=scale_sb[:], op=MULT)
+            if i < EARLY:
+                nc.vector.tensor_tensor(out=prod[i][:, k, :], in0=codes_in[:, i // 2, 2 * (i % 2) + k, :].bitcast(FP8), in1=scale_sb[:], op=MULT)
+            else:
+                nc.gpsimd.tensor_tensor(out=prod[i][:, k, :], in0=cast[i][:, k, :], in1=scale_sb[:], op=MULT)
 
         def do_turn(i):
-            if not 0 <= i < PAIRS:
+            if i >= PAIRS:
                 return
             x = ps_x.tile([P, 2, 2, P], F32, tag="x", name="xt_t")
             xt[i] = x
@@ -134,39 +145,40 @@ def tile_perspectronencodernetwork_pa_w8_kernel(
                     nc.tensor.transpose(x[:, r, u, :], pairs_of_k[:, 256 * r + u : 256 * (r + 1) : 2], ident[:])
 
         def do_group(i):
-            if not 0 <= i < PAIRS:
+            if i >= PAIRS:
                 return
             g = work.tile([P, 2 * P * 4], BF16, tag="xg", name="xg_t", align_bytes=64)
             xg[i] = g
-            dst = g[:].bitcast(F32).rearrange("p (r q u) -> p r q u", r=2, u=2)
-            src = xt[i][:].rearrange("p r u q -> p r q u")
-            if i == 0:
-                nc.vector.tensor_copy(out=dst, in_=src)
-            else:
-                nc.scalar.copy(out=dst, in_=src)
+            nc.scalar.copy(out=g[:].bitcast(F32).rearrange("p (r q u) -> p r q u", r=2, u=2), in_=xt[i][:].rearrange("p r u q -> p r q u"))
 
         def do_quant_x(i):
-            if not 0 <= i < PAIRS:
+            if i >= PAIRS:
                 return
             q = work.tile([P, 4 * 2 * P], U8, tag="xq", name="xq_t", align_bytes=64)
             s = work.tile([P, 2 * P], U8, tag="xs", name="xs_t", align_bytes=64)
             xq[i], xs[i] = q, s
             nc.vector.quantize_mx(out=q[:].bitcast(FP8X4), scales=s[:], in_=xg[i][:])
 
-        def do_group_v(b, t):
-            if not 0 <= b < SETS:
+        def do_group_v(j, k):
+            if j >= PAIRS:
                 return
+            b, t = j // 2, 2 * (j % 2) + k
             if t == 0:
-                g = work.tile([P, 4, P, 4], BF16, tag="vg", name="vg_t", align_bytes=64)
+                g = vwork.tile([P, 4, P, 4], BF16, tag="vg", name="vg_t", align_bytes=64)
                 vg[b] = g
-            nc.scalar.copy(out=vg[b][:, t], in_=vraw[:, b].rearrange("p j (m t) -> p t m j", t=4)[:, t])
+            src = vraw[:, b].rearrange("p j (m t) -> p t m j", t=4)[:, t]
+            if b == 0 and t >= 2 or b == 1 and t >= 2:
+                nc.vector.tensor_copy(out=vg[b][:, t], in_=src)
+            else:
+                nc.scalar.copy(out=vg[b][:, t], in_=src)
 
-        def do_quant_v(b, half):
-            if not 0 <= b < SETS:
+        def do_quant_v(j):
+            if j >= PAIRS:
                 return
+            b, half = j // 2, j % 2
             if half == 0:
-                q = work.tile([P, 4 * FEATS], U8, tag="vq", name="vq_t", align_bytes=64)
-                s = work.tile([P, FEATS], U8, tag="vs", name="vs_t", align_bytes=64)
+                q = vwork.tile([P, 4 * FEATS], U8, tag="vq", name="vq_t", align_bytes=64)
+                s = vwork.tile([P, FEATS], U8, tag="vs", name="vs_t", align_bytes=64)
                 vq[b], vs[b] = q, s
             nc.vector.quantize_mx(
                 out=vq[b][:, 1024 * half : 1024 * (half + 1)].bitcast(FP8X4),
@@ -174,113 +186,142 @@ def tile_perspectronencodernetwork_pa_w8_kernel(
                 in_=vg[b][:, 2 * half : 2 * half + 2].rearrange("p t m j -> p (t m j)"),
             )
 
-        def do_mix(i):
-            if not 0 <= i < PAIRS:
+        def do_mix(i, r):
+            if i >= PAIRS:
                 return
             b = i // 2
-            for r in range(2):
-                h = ps_h.tile([P, 4, P], F32, tag="h", name="h_t")
-                hps[(i, r)] = h
-                for t in range(4):
-                    nc.tensor.matmul_mx(
-                        out=h[:, t, :],
-                        lhsT=vq[b][:, 512 * t : 512 * (t + 1)].bitcast(FP8X4),
-                        lhsT_scale=vs[b][:, P * t : P * (t + 1)],
-                        rhs=xq[i][:, 512 * r : 512 * (r + 1)].bitcast(FP8X4),
-                        rhs_scale=xs[i][:, P * r : P * (r + 1)],
-                        start=True, stop=True,
-                    )
+            h = ps_h.tile([P, 4, P], F32, tag="h", name="h_t")
+            hps[(i, r)] = h
+            for t in range(4):
+                nc.tensor.matmul_mx(
+                    out=h[:, t, :],
+                    lhsT=vq[b][:, 512 * t : 512 * (t + 1)].bitcast(FP8X4),
+                    lhsT_scale=vs[b][:, P * t : P * (t + 1)],
+                    rhs=xq[i][:, 512 * r : 512 * (r + 1)].bitcast(FP8X4),
+                    rhs_scale=xs[i][:, P * r : P * (r + 1)],
+                    start=True, stop=True,
+                )
 
-        def do_relu(i):
-            if not 0 <= i < PAIRS:
+        def do_relu(i, r):
+            if i >= PAIRS:
                 return
-            g = work.tile([P, 2, P, 4], BF16, tag="hg", name="hg_t", align_bytes=64)
-            hg[i] = g
-            for r in range(2):
-                nc.scalar.activation(out=g[:, r], in_=hps[(i, r)][:].rearrange("p t q -> p q t"), func=RELU)
+            if r == 0:
+                g = work.tile([P, 2, P, 4], BF16, tag="hg", name="hg_t", align_bytes=64)
+                hg[i] = g
+            nc.scalar.activation(out=hg[i][:, r], in_=hps[(i, r)][:].rearrange("p t q -> p q t"), func=RELU)
 
         def do_quant_h(i):
-            if not 0 <= i < PAIRS:
+            if i >= PAIRS:
                 return
             q = work.tile([P, 4 * 2 * P], U8, tag="hq", name="hq_t", align_bytes=64)
             s = work.tile([P, 2 * P], U8, tag="hs", name="hs_t", align_bytes=64)
             hq[i], hs[i] = q, s
             nc.vector.quantize_mx(out=q[:].bitcast(FP8X4), scales=s[:], in_=hg[i][:].rearrange("p r q t -> p (r q t)"))
 
-        def do_project(i, w):
-            if not 0 <= i < PAIRS:
-                return
-            banks = []
-            for r in range(2):
-                o = ps_out.tile([P, FEATS], F32, tag="o", name="o_t")
-                banks.append(o)
-                nc.tensor.matmul_mx(
-                    out=o[:],
-                    lhsT=hq[i][:, 512 * r : 512 * (r + 1)].bitcast(FP8X4),
-                    lhsT_scale=hs[i][:, P * r : P * (r + 1)],
-                    rhs=w_sb[:, w, :].bitcast(FP8X4),
-                    rhs_scale=wscale_sb[:, FEATS * w : FEATS * (w + 1)],
-                    start=True, stop=True,
-                )
-            y = stores.tile([P, 2, FEATS], F32, tag="y%d" % w, name="y_t")
-            for r in range(2):
-                if r == 1 and w < 2 and i >= LATE:
-                    z = work.tile([P, FEATS], F32, tag="z", name="z_t")
-                    nc.scalar.copy(out=z[:], in_=banks[r][:])
-                    nc.gpsimd.tensor_tensor(out=y[:, r, :], in0=z[:], in1=bias_sb[:, w, :], op=ADD)
-                else:
-                    nc.vector.tensor_tensor(out=y[:, r, :], in0=banks[r][:], in1=bias_sb[:, w, :], op=ADD)
+        def do_project(i, k):
+            w, r = k // 2, k % 2
+            o = ps_out.tile([P, FEATS], F32, tag="o", name="o_t")
+            bank[(i, k)] = o
+            nc.tensor.matmul_mx(
+                out=o[:],
+                lhsT=hq[i][:, 512 * r : 512 * (r + 1)].bitcast(FP8X4),
+                lhsT_scale=hs[i][:, P * r : P * (r + 1)],
+                rhs=w_sb[:, w, :].bitcast(FP8X4),
+                rhs_scale=wscale_sb[:, FEATS * w : FEATS * (w + 1)],
+                start=True, stop=True,
+            )
+
+        def store(i, k):
+            w, r = k // 2, k % 2
             h = 2 * (i % 2)
             rows = outs[w][i // 2].rearrange("(p r) n -> p r n", r=4)
+            y = res[(i, w)]
             if i == PAIRS - 1 and w == 2:
-                for r in range(2):
-                    nc.sync.dma_start(out=rows[:, h + r, :], in_=y[:, r, :])
-            else:
+                nc.sync.dma_start(out=rows[:, h + r, :], in_=y[:, r, :])
+            elif (i, w) in done:
                 nc.sync.dma_start(out=rows[:, h : h + 2, :], in_=y[:])
+            done[(i, w)] = True
 
-        do_prod(0)
-        do_turn(0)
-        for t in range(4):
-            do_group_v(0, t)
+        def do_add(i, k):
+            w, r = k // 2, k % 2
+            if (i, w) not in res:
+                y = stores.tile([P, 2, FEATS], F32, tag="y%d" % w, name="y_t")
+                res[(i, w)] = y
+            if k in SHARED.get(i, ()):
+                z = work.tile([P, FEATS], F32, tag="z", name="z_t")
+                nc.scalar.copy(out=z[:], in_=bank[(i, k)][:])
+                bank[(i, k)] = z
+            else:
+                nc.vector.tensor_tensor(out=res[(i, w)][:, r, :], in0=bank[(i, k)][:], in1=bias_sb[:, w, :], op=ADD)
+                store(i, k)
+
+        def do_late_add(i, k):
+            if k in SHARED.get(i, ()):
+                w, r = k // 2, k % 2
+                nc.gpsimd.tensor_tensor(out=res[(i, w)][:, r, :], in0=bank[(i, k)][:], in1=bias_sb[:, w, :], op=ADD)
+                store(i, k)
+
+        do_prod(0, 0)
+        do_prod(0, 1)
+        do_group_v(0, 0)
+        do_group_v(0, 1)
         do_prod(1, 0)
+        do_group_v(1, 0)
+        do_group_v(1, 1)
+        do_turn(0)
+        do_quant_v(0)
+        do_quant_v(1)
         do_group(0)
-        do_prod(1, 1)
+        spread_biases(0, 2)
         do_quant_x(0)
+        do_prod(1, 1)
+        do_mix(0, 0)
+        do_mix(0, 1)
+        do_prod(2, 0)
         do_turn(1)
-        do_quant_v(0, 0)
-        do_quant_v(0, 1)
-        do_mix(0)
-        for w in range(3):
-            spread_bias(w)
-        do_prod(2)
-        do_relu(0)
+        do_relu(0, 0)
+        do_relu(0, 1)
         do_group(1)
-        do_cast(3)
-        do_quant_x(1)
+        do_prod(3, 0)
+        do_prod(3, 1)
         do_quant_h(0)
-        do_mix(1)
-        do_prod(3)
-        for t in range(4):
-            do_group_v(1, t)
-        do_turn(2)
-        do_group(2)
-        do_cast(4)
-        do_quant_v(1, 0)
-        do_quant_v(1, 1)
+        do_prod(2, 1)
+        do_group_v(2, 0)
+        spread_biases(2, 3)
+        do_quant_x(1)
+        do_group_v(3, 0)
+        do_group_v(3, 1)
+        do_group_v(2, 1)
 
         for i in range(PAIRS):
-            do_relu(i + 1)
-            do_quant_x(i + 2)
             do_project(i, 0)
-            do_turn(i + 3)
-            do_group(i + 3)
-            do_quant_h(i + 1)
             do_project(i, 1)
-            b = i // 2 + 2
-            for t in (0, 1) if i % 2 == 0 else (2, 3):
-                do_group_v(b, t)
+            do_mix(i + 1, 0)
             do_project(i, 2)
-            do_mix(i + 2)
-            do_quant_v(b, i % 2)
-            do_cast(i + 5)
-            do_prod(i + 4)
+            do_add(i, 0)
+            do_mix(i + 1, 1)
+            do_add(i, 1)
+            do_project(i, 3)
+            do_add(i, 2)
+            do_late_add(i, 1)
+            do_add(i, 3)
+            do_relu(i + 1, 0)
+            do_relu(i + 1, 1)
+            do_turn(i + 2)
+            do_group(i + 2)
+            do_group_v(i + 4, 0)
+            do_project(i, 4)
+            do_quant_h(i + 1)
+            do_cast(i + 4)
+            if i % 2 == 0:
+                do_quant_v(i + 2)
+            do_project(i, 5)
+            do_quant_x(i + 2)
+            do_prod(i + 4, 0)
+            do_prod(i + 4, 1)
+            if i % 2 == 0:
+                do_quant_v(i + 3)
+            do_group_v(i + 4, 1)
+            do_add(i, 4)
+            do_add(i, 5)
+            do_late_add(i, 5)

@@ -19,7 +19,7 @@ RELU = mybir.ActivationFunctionType.Relu
 
 P = 128
 PAIRS = 2 * SETS
-EARLY = 4
+EARLY = 3
 SHARED = {9: (1, 5), 10: (1,), 11: (1, 5)}
 
 
@@ -83,15 +83,15 @@ def tile_perspectronencodernetwork_pa_w8_kernel(
 
         load_codes(0, 1)
         load_v(0, 1)
-        load_wscales(0)
-        load_wscales(1)
-        load_codes(1, 2)
-        load_words(0)
-        load_words(1)
-        load_wscales(2)
-        load_words(2)
         load_v(1, 2)
+        load_codes(1, 2)
+        load_wscales(0)
+        load_words(0)
+        load_wscales(1)
+        load_words(1)
         load_codes(2, 3)
+        load_words(2)
+        load_wscales(2)
         load_v(2, 3)
         load_codes(3, 6)
         load_v(3, 6)
@@ -108,7 +108,7 @@ def tile_perspectronencodernetwork_pa_w8_kernel(
             ps = ps_out.tile([P, 2, FEATS], BF16, tag="o", name="bias_ps")
             for w in range(w0, w1):
                 nc.tensor.matmul(ps[:, w - w0, :], lhsT=ones[:], rhs=bias_rows[:, FEATS * w : FEATS * (w + 1)], start=True, stop=True)
-            nc.scalar.copy(out=bias_sb[:, w0:w1, :], in_=ps[:, : w1 - w0, :])
+            (nc.vector.tensor_copy if w0 else nc.scalar.copy)(out=bias_sb[:, w0:w1, :], in_=ps[:, : w1 - w0, :])
 
         cast, prod, xt, xg, xq, xs = {}, {}, {}, {}, {}, {}
         vg, vq, vs = {}, {}, {}
@@ -149,7 +149,7 @@ def tile_perspectronencodernetwork_pa_w8_kernel(
                 return
             g = work.tile([P, 2 * P * 4], BF16, tag="xg", name="xg_t", align_bytes=64)
             xg[i] = g
-            nc.scalar.copy(out=g[:].bitcast(F32).rearrange("p (r q u) -> p r q u", r=2, u=2), in_=xt[i][:].rearrange("p r u q -> p r q u"))
+            (nc.vector.tensor_copy if i == 1 else nc.scalar.copy)(out=g[:].bitcast(F32).rearrange("p (r q u) -> p r q u", r=2, u=2), in_=xt[i][:].rearrange("p r u q -> p r q u"))
 
         def do_quant_x(i):
             if i >= PAIRS:
@@ -167,7 +167,7 @@ def tile_perspectronencodernetwork_pa_w8_kernel(
                 g = vwork.tile([P, 4, P, 4], BF16, tag="vg", name="vg_t", align_bytes=64)
                 vg[b] = g
             src = vraw[:, b].rearrange("p j (m t) -> p t m j", t=4)[:, t]
-            if b == 0 and t >= 2 or b == 1 and t >= 2:
+            if b < 2 and t == 3:
                 nc.vector.tensor_copy(out=vg[b][:, t], in_=src)
             else:
                 nc.scalar.copy(out=vg[b][:, t], in_=src)
@@ -265,33 +265,34 @@ def tile_perspectronencodernetwork_pa_w8_kernel(
         do_prod(0, 1)
         do_group_v(0, 0)
         do_group_v(0, 1)
+        do_turn(0)
         do_prod(1, 0)
+        do_prod(1, 1)
         do_group_v(1, 0)
         do_group_v(1, 1)
-        do_turn(0)
         do_quant_v(0)
-        do_quant_v(1)
         do_group(0)
         spread_biases(0, 2)
+        do_turn(1)
         do_quant_x(0)
-        do_prod(1, 1)
+        do_quant_v(1)
         do_mix(0, 0)
         do_mix(0, 1)
-        do_prod(2, 0)
-        do_turn(1)
+        do_group_v(2, 0)
+        do_group_v(3, 1)
+        do_group(1)
         do_relu(0, 0)
         do_relu(0, 1)
-        do_group(1)
+        do_prod(2, 0)
+        do_cast(3)
+        do_quant_x(1)
+        do_quant_h(0)
+        spread_biases(2, 3)
+        do_prod(2, 1)
+        do_group_v(3, 0)
+        do_group_v(2, 1)
         do_prod(3, 0)
         do_prod(3, 1)
-        do_quant_h(0)
-        do_prod(2, 1)
-        do_group_v(2, 0)
-        spread_biases(2, 3)
-        do_quant_x(1)
-        do_group_v(3, 0)
-        do_group_v(3, 1)
-        do_group_v(2, 1)
 
         for i in range(PAIRS):
             do_project(i, 0)
@@ -301,9 +302,9 @@ def tile_perspectronencodernetwork_pa_w8_kernel(
             do_add(i, 0)
             do_mix(i + 1, 1)
             do_add(i, 1)
+            do_late_add(i, 1)
             do_project(i, 3)
             do_add(i, 2)
-            do_late_add(i, 1)
             do_add(i, 3)
             do_relu(i + 1, 0)
             do_relu(i + 1, 1)

@@ -20,7 +20,7 @@ RELU = mybir.ActivationFunctionType.Relu
 P = 128
 PAIRS = 2 * SETS
 EARLY = 3
-SHARED = {9: (1, 5), 10: (1,), 11: (1, 5)}
+SHARED = {9: (1,), 10: (1,), 11: (1, 5)}
 
 
 def tile_perspectronencodernetwork_pa_w8_kernel(
@@ -162,15 +162,17 @@ def tile_perspectronencodernetwork_pa_w8_kernel(
         def do_group_v(j, k):
             if j >= PAIRS:
                 return
-            b, t = j // 2, 2 * (j % 2) + k
-            if t == 0:
+            b, quarter = j // 2, 2 * (j % 2) + k
+            if quarter == 0:
                 g = vwork.tile([P, 4, P, 4], BF16, tag="vg", name="vg_t", align_bytes=64)
                 vg[b] = g
-            src = vraw[:, b].rearrange("p j (m t) -> p t m j", t=4)[:, t]
-            if b < 2 and t == 3:
-                nc.vector.tensor_copy(out=vg[b][:, t], in_=src)
+            m = slice(32 * quarter, 32 * (quarter + 1))
+            src = vraw[:, b].rearrange("p j (m t) -> p m t j", t=4)[:, m]
+            dst = vg[b][:].rearrange("p t m j -> p m t j")[:, m]
+            if b < 2 and quarter == 3:
+                nc.vector.tensor_copy(out=dst, in_=src)
             else:
-                nc.scalar.copy(out=vg[b][:, t], in_=src)
+                nc.scalar.copy(out=dst, in_=src)
 
         def do_quant_v(j):
             if j >= PAIRS:
@@ -272,25 +274,25 @@ def tile_perspectronencodernetwork_pa_w8_kernel(
         do_group_v(1, 1)
         do_quant_v(0)
         do_group(0)
-        spread_biases(0, 2)
-        do_turn(1)
         do_quant_x(0)
         do_quant_v(1)
+        spread_biases(0, 2)
+        do_turn(1)
         do_mix(0, 0)
         do_mix(0, 1)
         do_group_v(2, 0)
-        do_group_v(3, 1)
         do_group(1)
         do_relu(0, 0)
         do_relu(0, 1)
         do_prod(2, 0)
         do_cast(3)
-        do_quant_x(1)
-        do_quant_h(0)
-        spread_biases(2, 3)
         do_prod(2, 1)
-        do_group_v(3, 0)
+        do_quant_h(0)
+        do_group_v(3, 1)
+        spread_biases(2, 3)
+        do_quant_x(1)
         do_group_v(2, 1)
+        do_group_v(3, 0)
         do_prod(3, 0)
         do_prod(3, 1)
 

from contextlib import ExitStack

import concourse.mybir as mybir
from concourse.masks import make_identity

SETS, POINTS, FEATS = 6, 512, 512
FLOPS = 2 * SETS * POINTS * FEATS * (POINTS + 3 * FEATS)

F32 = mybir.dt.float32
BF16 = mybir.dt.bfloat16
U8 = mybir.dt.uint8
I32 = mybir.dt.int32
FP8 = mybir.dt.float8_e4m3fn
FP8X4 = mybir.dt.float8_e4m3fn_x4
ADD = mybir.AluOpType.add
MULT = mybir.AluOpType.mult
COPY = mybir.ActivationFunctionType.Copy
RELU = mybir.ActivationFunctionType.Relu

P = 128
PAIRS = 2 * SETS
EARLY = 3
SHARED = {9: (1,), 10: (1,), 11: (1, 5)}


def tile_perspectronencodernetwork_pa_w8_kernel(
    tc, attn1_bytes, attn1_scale, v1,
    wq_words, wq_scales, bq, wk_words, wk_scales, bk, wv_words, wv_scales, bv,
    out_0, out_1, out_2,
):
    nc = tc.nc
    outs = [out_0, out_1, out_2]
    words_in = [wq_words, wk_words, wv_words]
    wscales_in = [wq_scales, wk_scales, wv_scales]
    biases_in = [bq, bk, bv]

    with ExitStack() as ctx:
        keep = ctx.enter_context(tc.tile_pool(name="keep", bufs=1))
        work = ctx.enter_context(tc.tile_pool(name="work", bufs=4))
        vwork = ctx.enter_context(tc.tile_pool(name="vwork", bufs=3))
        stores = ctx.enter_context(tc.tile_pool(name="stores", bufs=5))
        ps_out = ctx.enter_context(tc.psum_pool(name="ps_out", bufs=4))
        ps_h = ctx.enter_context(tc.psum_pool(name="ps_h", bufs=2))
        ps_x = ctx.enter_context(tc.psum_pool(name="ps_x", bufs=2))
        ctx.enter_context(tc.manual_schedule())

        ident = keep.tile([P, P], F32)
        make_identity(nc, ident[:])
        bias_rows = keep.tile([P, 3 * FEATS], BF16)
        nc.vector.memset(bias_rows[:].bitcast(F32), 0.0)
        wscale_sb = keep.tile([P, 3 * FEATS], U8, align_bytes=64)
        nc.vector.memset(wscale_sb[:].bitcast(I32), 0)
        warm = keep.tile([P, 1], F32)
        nc.vector.memset(warm[:], 0.0)
        ones = keep.tile([P, P], BF16)
        nc.vector.memset(ones[:], 1.0)

        for w in range(3):
            nc.scalar.dma_start(out=bias_rows[0:1, FEATS * w : FEATS * (w + 1)], in_=biases_in[w].rearrange("(o n) -> o n", o=1))
        warm_out = keep.tile([P, 1], F32)
        nc.scalar.activation(out=warm_out[:], in_=warm[:], func=RELU)
        scale_col = keep.tile([P, 4], F32)
        nc.sync.dma_start(out=scale_col[:], in_=attn1_scale.rearrange("a b (p t) -> p (a b t)", t=4))
        codes_in = keep.tile([P, SETS, 4, POINTS], U8, align_bytes=64)
        vraw = keep.tile([P, SETS, 4, FEATS], BF16, align_bytes=64)
        w_sb = keep.tile([P, 3, 4 * FEATS], U8, align_bytes=64)

        def load_codes(b0, b1):
            nc.sync.dma_start(out=codes_in[:, b0:b1], in_=attn1_bytes[b0:b1].rearrange("b (p r) s -> p b r s", r=4))

        def load_v(b0, b1):
            nc.sync.dma_start(out=vraw[:, b0:b1], in_=v1[b0:b1].rearrange("b (p j) f -> p b j f", j=4))

        def load_words(w):
            nc.sync.dma_start(out=w_sb[:, w, :], in_=words_in[w][0].rearrange("p n t -> p (n t)"))

        def load_wscales(w):
            for quad in range(4):
                nc.sync.dma_start(
                    out=wscale_sb[32 * quad : 32 * quad + 4, FEATS * w : FEATS * (w + 1)].bitcast(I32),
                    in_=wscales_in[w][0, 4 * quad : 4 * quad + 4, :].bitcast(I32),
                )

        load_codes(0, 1)
        load_v(0, 1)
        load_v(1, 2)
        load_codes(1, 2)
        load_wscales(0)
        load_words(0)
        load_wscales(1)
        load_words(1)
        load_codes(2, 3)
        load_words(2)
        load_wscales(2)
        load_v(2, 3)
        load_codes(3, 6)
        load_v(3, 6)

        scale_ps = ps_x.tile([P, 4, P], F32, tag="x")
        for t in range(4):
            nc.tensor.transpose(scale_ps[:, t, :], scale_col[:, t : t + 1].to_broadcast([P, P]), ident[:])
        scale_sb = keep.tile([P, POINTS], F32)
        nc.scalar.copy(out=scale_sb[:].rearrange("q (p t) -> q p t", t=4), in_=scale_ps[:].rearrange("q t p -> q p t"))

        bias_sb = keep.tile([P, 3, FEATS], BF16)

        def spread_biases(w0, w1):
            ps = ps_out.tile([P, 2, FEATS], BF16, tag="o", name="bias_ps")
            for w in range(w0, w1):
                nc.tensor.matmul(ps[:, w - w0, :], lhsT=ones[:], rhs=bias_rows[:, FEATS * w : FEATS * (w + 1)], start=True, stop=True)
            (nc.vector.tensor_copy if w0 else nc.scalar.copy)(out=bias_sb[:, w0:w1, :], in_=ps[:, : w1 - w0, :])

        cast, prod, xt, xg, xq, xs = {}, {}, {}, {}, {}, {}
        vg, vq, vs = {}, {}, {}
        hps, hg, hq, hs = {}, {}, {}, {}
        bank, res, done = {}, {}, {}

        def do_cast(i):
            if i >= PAIRS:
                return
            c = work.tile([P, 2, POINTS], BF16, tag="cast", name="cast_t")
            cast[i] = c
            h = 2 * (i % 2)
            nc.scalar.copy(out=c[:], in_=codes_in[:, i // 2, h : h + 2, :].bitcast(FP8))

        def do_prod(i, k):
            if i >= PAIRS:
                return
            if k == 0:
                y = work.tile([P, 2, POINTS], BF16, tag="prod", name="prod_t", align_bytes=64)
                prod[i] = y
            if i < EARLY:
                nc.vector.tensor_tensor(out=prod[i][:, k, :], in0=codes_in[:, i // 2, 2 * (i % 2) + k, :].bitcast(FP8), in1=scale_sb[:], op=MULT)
            else:
                nc.gpsimd.tensor_tensor(out=prod[i][:, k, :], in0=cast[i][:, k, :], in1=scale_sb[:], op=MULT)

        def do_turn(i):
            if i >= PAIRS:
                return
            x = ps_x.tile([P, 2, 2, P], F32, tag="x", name="xt_t")
            xt[i] = x
            pairs_of_k = prod[i][:].rearrange("p r s -> p (r s)").bitcast(F32)
            for r in range(2):
                for u in range(2):
                    nc.tensor.transpose(x[:, r, u, :], pairs_of_k[:, 256 * r + u : 256 * (r + 1) : 2], ident[:])

        def do_group(i):
            if i >= PAIRS:
                return
            g = work.tile([P, 2 * P * 4], BF16, tag="xg", name="xg_t", align_bytes=64)
            xg[i] = g
            (nc.vector.tensor_copy if i == 1 else nc.scalar.copy)(out=g[:].bitcast(F32).rearrange("p (r q u) -> p r q u", r=2, u=2), in_=xt[i][:].rearrange("p r u q -> p r q u"))

        def do_quant_x(i):
            if i >= PAIRS:
                return
            q = work.tile([P, 4 * 2 * P], U8, tag="xq", name="xq_t", align_bytes=64)
            s = work.tile([P, 2 * P], U8, tag="xs", name="xs_t", align_bytes=64)
            xq[i], xs[i] = q, s
            nc.vector.quantize_mx(out=q[:].bitcast(FP8X4), scales=s[:], in_=xg[i][:])

        def do_group_v(j, k):
            if j >= PAIRS:
                return
            b, quarter = j // 2, 2 * (j % 2) + k
            if quarter == 0:
                g = vwork.tile([P, 4, P, 4], BF16, tag="vg", name="vg_t", align_bytes=64)
                vg[b] = g
            m = slice(32 * quarter, 32 * (quarter + 1))
            src = vraw[:, b].rearrange("p j (m t) -> p m t j", t=4)[:, m]
            dst = vg[b][:].rearrange("p t m j -> p m t j")[:, m]
            if b < 2 and quarter == 3:
                nc.vector.tensor_copy(out=dst, in_=src)
            else:
                nc.scalar.copy(out=dst, in_=src)

        def do_quant_v(j):
            if j >= PAIRS:
                return
            b, half = j // 2, j % 2
            if half == 0:
                q = vwork.tile([P, 4 * FEATS], U8, tag="vq", name="vq_t", align_bytes=64)
                s = vwork.tile([P, FEATS], U8, tag="vs", name="vs_t", align_bytes=64)
                vq[b], vs[b] = q, s
            nc.vector.quantize_mx(
                out=vq[b][:, 1024 * half : 1024 * (half + 1)].bitcast(FP8X4),
                scales=vs[b][:, 256 * half : 256 * (half + 1)],
                in_=vg[b][:, 2 * half : 2 * half + 2].rearrange("p t m j -> p (t m j)"),
            )

        def do_mix(i, r):
            if i >= PAIRS:
                return
            b = i // 2
            h = ps_h.tile([P, 4, P], F32, tag="h", name="h_t")
            hps[(i, r)] = h
            for t in range(4):
                nc.tensor.matmul_mx(
                    out=h[:, t, :],
                    lhsT=vq[b][:, 512 * t : 512 * (t + 1)].bitcast(FP8X4),
                    lhsT_scale=vs[b][:, P * t : P * (t + 1)],
                    rhs=xq[i][:, 512 * r : 512 * (r + 1)].bitcast(FP8X4),
                    rhs_scale=xs[i][:, P * r : P * (r + 1)],
                    start=True, stop=True,
                )

        def do_relu(i, r):
            if i >= PAIRS:
                return
            if r == 0:
                g = work.tile([P, 2, P, 4], BF16, tag="hg", name="hg_t", align_bytes=64)
                hg[i] = g
            nc.scalar.activation(out=hg[i][:, r], in_=hps[(i, r)][:].rearrange("p t q -> p q t"), func=RELU)

        def do_quant_h(i):
            if i >= PAIRS:
                return
            q = work.tile([P, 4 * 2 * P], U8, tag="hq", name="hq_t", align_bytes=64)
            s = work.tile([P, 2 * P], U8, tag="hs", name="hs_t", align_bytes=64)
            hq[i], hs[i] = q, s
            nc.vector.quantize_mx(out=q[:].bitcast(FP8X4), scales=s[:], in_=hg[i][:].rearrange("p r q t -> p (r q t)"))

        def do_project(i, k):
            w, r = k // 2, k % 2
            o = ps_out.tile([P, FEATS], F32, tag="o", name="o_t")
            bank[(i, k)] = o
            nc.tensor.matmul_mx(
                out=o[:],
                lhsT=hq[i][:, 512 * r : 512 * (r + 1)].bitcast(FP8X4),
                lhsT_scale=hs[i][:, P * r : P * (r + 1)],
                rhs=w_sb[:, w, :].bitcast(FP8X4),
                rhs_scale=wscale_sb[:, FEATS * w : FEATS * (w + 1)],
                start=True, stop=True,
            )

        def store(i, k):
            w, r = k // 2, k % 2
            h = 2 * (i % 2)
            rows = outs[w][i // 2].rearrange("(p r) n -> p r n", r=4)
            y = res[(i, w)]
            if i == PAIRS - 1 and w == 2:
                nc.sync.dma_start(out=rows[:, h + r, :], in_=y[:, r, :])
            elif (i, w) in done:
                nc.sync.dma_start(out=rows[:, h : h + 2, :], in_=y[:])
            done[(i, w)] = True

        def do_add(i, k):
            w, r = k // 2, k % 2
            if (i, w) not in res:
                y = stores.tile([P, 2, FEATS], F32, tag="y%d" % w, name="y_t")
                res[(i, w)] = y
            if k in SHARED.get(i, ()):
                z = work.tile([P, FEATS], F32, tag="z", name="z_t")
                nc.scalar.copy(out=z[:], in_=bank[(i, k)][:])
                bank[(i, k)] = z
            else:
                nc.vector.tensor_tensor(out=res[(i, w)][:, r, :], in0=bank[(i, k)][:], in1=bias_sb[:, w, :], op=ADD)
                store(i, k)

        def do_late_add(i, k):
            if k in SHARED.get(i, ()):
                w, r = k // 2, k % 2
                nc.gpsimd.tensor_tensor(out=res[(i, w)][:, r, :], in0=bank[(i, k)][:], in1=bias_sb[:, w, :], op=ADD)
                store(i, k)

        do_prod(0, 0)
        do_prod(0, 1)
        do_group_v(0, 0)
        do_group_v(0, 1)
        do_turn(0)
        do_prod(1, 0)
        do_prod(1, 1)
        do_group_v(1, 0)
        do_group_v(1, 1)
        do_quant_v(0)
        do_group(0)
        do_quant_x(0)
        do_quant_v(1)
        spread_biases(0, 2)
        do_turn(1)
        do_mix(0, 0)
        do_mix(0, 1)
        do_group_v(2, 0)
        do_group(1)
        do_relu(0, 0)
        do_relu(0, 1)
        do_prod(2, 0)
        do_cast(3)
        do_prod(2, 1)
        do_quant_h(0)
        do_group_v(3, 1)
        spread_biases(2, 3)
        do_quant_x(1)
        do_group_v(2, 1)
        do_group_v(3, 0)
        do_prod(3, 0)
        do_prod(3, 1)

        for i in range(PAIRS):
            do_project(i, 0)
            do_project(i, 1)
            do_mix(i + 1, 0)
            do_project(i, 2)
            do_add(i, 0)
            do_mix(i + 1, 1)
            do_add(i, 1)
            do_late_add(i, 1)
            do_project(i, 3)
            do_add(i, 2)
            do_add(i, 3)
            do_relu(i + 1, 0)
            do_relu(i + 1, 1)
            do_turn(i + 2)
            do_group(i + 2)
            do_group_v(i + 4, 0)
            do_project(i, 4)
            do_quant_h(i + 1)
            do_cast(i + 4)
            if i % 2 == 0:
                do_quant_v(i + 2)
            do_project(i, 5)
            do_quant_x(i + 2)
            do_prod(i + 4, 0)
            do_prod(i + 4, 1)
            if i % 2 == 0:
                do_quant_v(i + 3)
            do_group_v(i + 4, 1)
            do_add(i, 4)
            do_add(i, 5)
            do_late_add(i, 5)
